import numpy as np
import ml_dtypes


def mxq(x, axis, fmt="e4m3"):
    dtype, down = {"e4m3": (ml_dtypes.float8_e4m3fn, 7), "e5m2": (ml_dtypes.float8_e5m2, 14)}[fmt]
    v = np.moveaxis(np.asarray(x, np.float32).astype(ml_dtypes.bfloat16).astype(np.float64), axis, -1)
    blocks = v.reshape(v.shape[:-1] + (-1, 32))
    amax = np.abs(blocks).max(-1, keepdims=True)
    byte = np.maximum(np.where(amax > 0, np.frexp(amax)[1] - 1 + 127, 0) - down, 1)
    scale = np.exp2(byte - 127.0)
    codes = (blocks / scale).astype(np.float32).astype(dtype).astype(np.float64)
    return np.moveaxis((codes * scale).reshape(v.shape), -1, axis)


WIDE = False


def mx_kscale(k):
    if not WIDE:
        return np.ones(k)
    levels = np.array([10, -10, 5, -5, 0])
    if k % 512:
        return np.exp2(np.random.permutation(np.resize(levels, k // 32))).repeat(32)
    a = np.empty((k // 512, 16))
    for p in range(k // 512):
        a[p, :8] = np.random.permutation(np.resize(levels, 8))
        for g in range(8):
            far = levels[np.abs(levels - a[p, g]) >= 10]
            a[p, g + 8] = far[np.random.randint(len(far))]
    return np.exp2(a.ravel()).repeat(32)


BF16 = ml_dtypes.bfloat16


def bf(x):
    return np.asarray(x, np.float32).astype(BF16)


def f64(x):
    return np.asarray(x).astype(np.float64)


E2M1 = np.array([0.0, 0.5, 1.0, 1.5, 2.0, 3.0, 4.0, 6.0, -0.0, -0.5, -1.0, -1.5, -2.0, -3.0, -4.0, -6.0])


def pack_weight(w, fmt):
    k, n = w.shape
    w = f64(bf(w)).reshape(k // 32, 32, n)
    amax = np.abs(w).max(1)
    if fmt == "e4m3":
        byte = np.frexp(amax)[1] - 1 + 127 - 7
    else:
        mant, ex = np.frexp(amax / 6.0)
        byte = np.where(mant > 0.5, ex, ex - 1) + 127
    byte = np.clip(np.where(amax > 0, byte, 1), 1, 254)
    scaled = (w * np.exp2(127.0 - byte)[:, None, :]).reshape(k, n).astype(np.float32)
    by_word = np.ascontiguousarray(scaled.reshape(k // 512, 128, 4, n).transpose(0, 1, 3, 2))
    if fmt == "e4m3":
        words = by_word.astype(ml_dtypes.float8_e4m3fn).view(np.uint8)
    else:
        c = by_word.astype(ml_dtypes.float4_e2m1fn).view(np.uint8) & 0xF
        words = c[..., 0::2] | (c[..., 1::2] << 4)
    return np.ascontiguousarray(words), np.ascontiguousarray(byte.astype(np.uint8).reshape(k // 512, 16, n))


def unpack_weight(words, scales, fmt):
    g, p, n, _ = words.shape
    if fmt == "e4m3":
        vals = np.ascontiguousarray(words).view(ml_dtypes.float8_e4m3fn).astype(np.float64)
    else:
        nib = np.empty((g, p, n, 4), np.uint8)
        nib[..., 0::2] = words & 0xF
        nib[..., 1::2] = words >> 4
        vals = E2M1[nib]
    vals = vals * np.repeat(np.exp2(scales.astype(np.float64) - 127.0), 8, axis=1)[..., None]
    return vals.transpose(0, 1, 3, 2).reshape(g * 512, n)


B, C, H, W, DM, GH = 6, 512, 32, 32, 128, 512


def sigmoid(v):
    return 1.0 / (1.0 + np.exp(-v))


def draw0():
    s = np.concatenate([mx_kscale(C), np.ones(C)])
    t = mx_kscale(GH)
    x = bf(np.random.standard_normal((B, C, H, W)) * s[:C][None, :, None, None])
    agg = bf(np.random.standard_normal((B, C, H, W)) * 0.7)
    g1w = np.random.standard_normal((GH, 2 * C)) / np.sqrt(2 * C) * t[:, None] / s[None, :]
    g1w_words, g1w_scales = pack_weight(np.ascontiguousarray(g1w.T), 'e4m3')
    g1b = bf(np.random.standard_normal(GH) * 0.3 * t)
    g2w = np.random.standard_normal((C, GH)) * 2.0 / np.sqrt(GH) / t[None, :]
    g2w_words, g2w_scales = pack_weight(np.ascontiguousarray(g2w.T), 'e4m3')
    g2b = bf(np.random.standard_normal(C) * 0.3)
    return {'x': x,
            'agg': agg,
            'g1w_words': g1w_words,
            'g1w_scales': g1w_scales,
            'g1b': g1b,
            'g2w_words': g2w_words,
            'g2w_scales': g2w_scales,
            'g2b': g2b}


def core(x, agg, g1w_words, g1w_scales, g1b, g2w_words, g2w_scales, g2b):
    a = f64(agg).reshape(B, C, H * W)
    cat = np.concatenate([f64(x).reshape(B, C, H * W), a], axis=1)
    hidden = np.maximum((unpack_weight(g1w_words, g1w_scales, 'e4m3').T @ mxq(cat, 1, 'e4m3')) + f64(g1b)[None, :, None], 0.0)
    gate = sigmoid((unpack_weight(g2w_words, g2w_scales, 'e4m3').T @ mxq(hidden, 1, 'e4m3')) + f64(g2b)[None, :, None])
    return (a * gate).reshape(B, C, H, W)


def e4m3fn_bytes(y):
    return np.clip(np.asarray(y, np.float64), -448.0, 448.0).astype(np.float32).astype(ml_dtypes.float8_e4m3fn).view(np.uint8)


def e4m3fn_values(b):
    return np.asarray(b, np.uint8).view(ml_dtypes.float8_e4m3fn).astype(np.float64)


def setup_inputs():
    d = draw0()
    x0 = np.asarray(d['x']).astype(np.float64)
    s = (np.max(np.abs(x0), axis=(0, 2, 3), keepdims=True) / 448.0).astype(np.float32)
    out = {}
    for k, v in d.items():
        if k == 'x':
            out['x_bytes'] = e4m3fn_bytes(x0 / s.astype(np.float64))
            out['x_scale'] = s
        else:
            out[k] = v
    return out


def reference(x_bytes, x_scale, agg, g1w_words, g1w_scales, g1b, g2w_words, g2w_scales, g2b):
    return core(e4m3fn_values(x_bytes) * x_scale.astype(np.float64), agg, g1w_words, g1w_scales, g1b, g2w_words, g2w_scales, g2b)

@@ -1,0 +1,237 @@
+from contextlib import ExitStack
+
+import concourse.mybir as mybir
+
+F32 = mybir.dt.float32
+BF16 = mybir.dt.bfloat16
+I32 = mybir.dt.int32
+U32 = mybir.dt.uint32
+U8 = mybir.dt.uint8
+FP8 = mybir.dt.float8_e4m3fn
+FP8X4 = mybir.dt.float8_e4m3fn_x4
+ACT = mybir.ActivationFunctionType
+ALU = mybir.AluOpType
+
+IMAGES, C, PIX = 6, 512, 1024
+P = 128
+PACK = 4
+N = 512
+WIDTHS = [256, 256, 512] + [512] * 8 + [512, 256, 256]
+GX = 352
+
+FLOPS = 2 * IMAGES * PIX * C * (2 * C + C)
+
+
+def tile_graphaugmentation_pb_t_w8_kernel(
+    tc, x_bytes, x_scale, agg, g1w_words, g1w_scales, g1b, g2w_words, g2w_scales, g2b, out
+):
+    nc = tc.nc
+    x_v = x_bytes.rearrange("b (p t) h w -> b p t (h w)", t=PACK)
+    agg_v = agg.rearrange("b (p t) h w -> b p t (h w)", t=PACK)
+    out_v = out.rearrange("b (p t) h w -> b p t (h w)", t=PACK)
+
+    chunks = []
+    pos = 0
+    for n in WIDTHS:
+        chunks.append((pos // PIX, pos % PIX, n))
+        pos += n
+    count = len(chunks)
+
+    with ExitStack() as ctx:
+        keep = ctx.enter_context(tc.tile_pool(name="keep", bufs=1))
+        work = ctx.enter_context(tc.tile_pool(name="work", bufs=2))
+        deep = ctx.enter_context(tc.tile_pool(name="deep", bufs=3))
+        outs = ctx.enter_context(tc.tile_pool(name="outs", bufs=4))
+        psum = ctx.enter_context(tc.psum_pool(name="psum", bufs=8))
+        ctx.enter_context(tc.manual_schedule())
+
+        xs = keep.tile([P, PACK], F32, name="xs")
+        b1 = keep.tile([P, PACK], BF16, name="b1")
+        b2 = keep.tile([P, PACK], BF16, name="b2")
+        nc.scalar.dma_start(out=xs[:], in_=x_scale.rearrange("o (p t) h w -> p (o t h w)", t=PACK))
+        nc.gpsimd.dma_start(out=b1[:], in_=g1b.rearrange("(p t) -> p t", t=PACK))
+        nc.gpsimd.dma_start(out=b2[:], in_=g2b.rearrange("(p t) -> p t", t=PACK))
+
+        s1_raw = keep.tile([P, C], U8, name="s1_raw", align_bytes=64)
+        s2_raw = keep.tile([P, C], U8, name="s2_raw", align_bytes=64)
+        nc.vector.memset(s1_raw[:].bitcast(I32), 0)
+        nc.vector.memset(s2_raw[:].bitcast(I32), 0)
+        dummy = keep.tile([P, 1], F32, name="dummy")
+        nc.vector.memset(dummy[:], 0.0)
+        nc.scalar.activation(out=dummy[:], in_=dummy[:], func=ACT.Sigmoid)
+
+        xb = [keep.tile([P, PACK, PIX], U8, name=f"xb{b}") for b in range(IMAGES)]
+        ag = [keep.tile([P, PACK, PIX], BF16, name=f"ag{b}") for b in range(IMAGES)]
+        w1_raw = [keep.tile([P, C], I32, name=f"w1_raw{g}", align_bytes=64) for g in range(2)]
+        w2_raw = keep.tile([P, C], I32, name="w2_raw", align_bytes=64)
+
+        def words(src):
+            return src.rearrange("p n t -> p (n t)").bitcast(I32)
+
+        def load(b, px):
+            nc.sync.dma_start(out=xb[b][:, :, px], in_=x_v[b][:, :, px])
+            nc.sync.dma_start(out=ag[b][:, :, px], in_=agg_v[b][:, :, px])
+
+        load(0, slice(0, 256))
+        load(0, slice(256, 512))
+        for q in range(4):
+            nc.sync.dma_start(
+                out=s1_raw[32 * q : 32 * q + 8, :].bitcast(I32), in_=g1w_scales[:, 4 * q : 4 * q + 4, :].bitcast(I32)
+            )
+        nc.sync.dma_start(out=w1_raw[0][:], in_=words(g1w_words[0]))
+        nc.sync.dma_start(out=w1_raw[1][:], in_=words(g1w_words[1]))
+        load(0, slice(512, PIX))
+        for q in range(4):
+            nc.sync.dma_start(
+                out=s2_raw[32 * q : 32 * q + 4, :].bitcast(I32), in_=g2w_scales[0, 4 * q : 4 * q + 4, :].bitcast(I32)
+            )
+        nc.sync.dma_start(out=w2_raw[:], in_=words(g2w_words[0]))
+        for b in range(1, IMAGES):
+            load(b, slice(0, PIX))
+
+        w1 = [keep.tile([P, C], I32, name=f"w1_{g}", align_bytes=64) for g in range(2)]
+        w2 = keep.tile([P, C], I32, name="w2", align_bytes=64)
+        s1 = keep.tile([P, C], U8, name="s1", align_bytes=64)
+        s2 = keep.tile([P, C], U8, name="s2", align_bytes=64)
+
+        def permute(dst, src):
+            nc.vector.tensor_copy(
+                out=dst[:].rearrange("p (t m) -> p t m", t=PACK), in_=src[:].rearrange("p (m t) -> p t m", t=PACK)
+            )
+
+        xw, xi, ai, xc, xsc, ac, asc, hp, hi, hc, hsc, gt, acc1, acc2 = ({} for _ in range(14))
+
+        def part(tiles, h):
+            b, px, n = chunks[h]
+            return tiles[b][:, :, px : px + n]
+
+        def widen(h, ts, scalar):
+            b, px, n = chunks[h]
+            if h not in xw:
+                xw[h] = work.tile([P, PACK, n], BF16, name="xw")
+            for t in ts:
+                src = xb[b][:, t, px : px + n].bitcast(FP8)
+                if scalar:
+                    nc.scalar.activation(out=xw[h][:, t, :], in_=src, func=ACT.Copy, scale=xs[:, t : t + 1])
+                else:
+                    nc.vector.tensor_scalar(
+                        out=xw[h][:, t, :], in0=src, scalar1=xs[:, t : t + 1], scalar2=None, op0=ALU.mult
+                    )
+
+        def inter(copy, dst, src, c0, c1):
+            if c1 > c0:
+                copy(
+                    out=dst[:, c0:c1, :].rearrange("p (c i) t -> p c t i", i=4),
+                    in_=src[:, :, c0:c1].rearrange("p t (c i) -> p c t i", i=4),
+                )
+
+        def x_pool(h):
+            return GX if 3 <= h and chunks[h][2] == N else 0
+
+        def width(h):
+            return chunks[h][2]
+
+        def grouped(h, pool, name):
+            return pool.tile([P, width(h), PACK], BF16, name=name, align_bytes=64)
+
+        def quant(codes, scales, h, src, name):
+            n = width(h)
+            codes[h] = deep.tile([P, n], U32, name=name + "c", align_bytes=64)
+            scales[h] = deep.tile([P, n], U8, name=name + "s", align_bytes=64)
+            nc.vector.quantize_mx(
+                out=codes[h][:].bitcast(FP8X4), scales=scales[h][:], in_=src[h][:].rearrange("p n t -> p (n t)")
+            )
+
+        def product(acc, h, t, weights, planes, codes, scales, start, stop):
+            m = slice(P * t, P * t + P)
+            nc.tensor.matmul_mx(
+                out=acc[:],
+                lhsT=weights[:, m].bitcast(FP8X4),
+                lhsT_scale=planes[:, m],
+                rhs=codes[h][:].bitcast(FP8X4),
+                rhs_scale=scales[h][:],
+                start=start,
+                stop=stop,
+            )
+
+        def mm1(h):
+            acc1[h] = []
+            for t in range(PACK):
+                acc = psum.tile([P, width(h)], F32, name="acc")
+                acc1[h].append(acc)
+                product(acc, h, t, w1[0], s1[:], xc, xsc, True, False)
+                product(acc, h, t, w1[1], s1[4:, :], ac, asc, False, True)
+
+        def mm2(h):
+            acc2[h] = []
+            for t in range(PACK):
+                acc = psum.tile([P, width(h)], F32, name="acc")
+                acc2[h].append(acc)
+                product(acc, h, t, w2, s2[:], hc, hsc, True, True)
+
+        def relu(h):
+            hp[h] = work.tile([P, PACK, width(h)], BF16, name="hp")
+            for t in range(PACK):
+                nc.scalar.activation(out=hp[h][:, t, :], in_=acc1[h][t][:], func=ACT.Relu, bias=b1[:, t : t + 1])
+
+        def sig(h):
+            gt[h] = outs.tile([P, PACK, width(h)], F32, name="gt")
+            for t in range(PACK):
+                nc.scalar.activation(out=gt[h][:, t, :], in_=acc2[h][t][:], func=ACT.Sigmoid, bias=b2[:, t : t + 1])
+
+        def store(h, ts):
+            b, px, n = chunks[h]
+            nc.sync.dma_start(out=out_v[b][:, ts, px : px + n], in_=gt[h][:, ts, :])
+
+        def prod(h, step):
+            src = part(ag, h)
+            for t in range(0, PACK, step):
+                ts = slice(t, t + step)
+                nc.vector.tensor_tensor(out=gt[h][:, ts, :], in0=gt[h][:, ts, :], in1=src[:, ts, :], op=ALU.mult)
+                if step == 1 and t % 2 == 1:
+                    store(h, slice(t - 1, t + 1))
+            if step > 1:
+                store(h, slice(0, PACK))
+
+        def on(h):
+            return 0 <= h < count
+
+        for i in range(-3, count + 1):
+            if on(i - 1):
+                sig(i - 1)
+            if on(i + 1):
+                quant(ac, asc, i + 1, ai, "a")
+                if i >= 0:
+                    mm1(i + 1)
+            if on(i + 2):
+                widen(i + 2, (0, 1, 2), False)
+            if on(i):
+                hi[i] = grouped(i, work, "hi")
+                hs = width(i) // 2 if i >= count - 2 else 0
+                inter(nc.vector.tensor_copy, hi[i], hp[i], 0, width(i) - hs)
+                inter(nc.scalar.copy, hi[i], hp[i], width(i) - hs, width(i))
+            if on(i + 2):
+                xi[i + 2] = grouped(i + 2, work, "xi")
+                inter(nc.vector.tensor_copy, xi[i + 2], xw[i + 2], 0, width(i + 2))
+            if on(i + 1) and i >= 0:
+                relu(i + 1)
+            if on(i + 3):
+                widen(i + 3, (3,), True)
+                ai[i + 3] = grouped(i + 3, deep, "ai")
+                inter(nc.scalar.copy, ai[i + 3], part(ag, i + 3), 0, width(i + 3))
+            if on(i):
+                quant(hc, hsc, i, hi, "h")
+                mm2(i)
+            if on(i - 1):
+                prod(i - 1, 1 if i >= count - 1 else 4)
+            if on(i + 2):
+                quant(xc, xsc, i + 2, xi, "x")
+            if i == -1:
+                permute(s1, s1_raw)
+                permute(w1[0], w1_raw[0])
+                permute(w1[1], w1_raw[1])
+                mm1(0)
+                relu(0)
+            if i == -1:
+                permute(s2, s2_raw)
+                permute(w2, w2_raw)

@@ -1,6 +1,7 @@
 from contextlib import ExitStack
 
 import concourse.mybir as mybir
+from concourse.masks import make_identity
 
 F32 = mybir.dt.float32
 BF16 = mybir.dt.bfloat16
@@ -42,7 +43,8 @@ def tile_graphaugmentation_pb_t_w8_kernel(
         work = ctx.enter_context(tc.tile_pool(name="work", bufs=2))
         deep = ctx.enter_context(tc.tile_pool(name="deep", bufs=3))
         outs = ctx.enter_context(tc.tile_pool(name="outs", bufs=4))
-        psum = ctx.enter_context(tc.psum_pool(name="psum", bufs=8))
+        psum = ctx.enter_context(tc.psum_pool(name="psum", bufs=6))
+        psa = ctx.enter_context(tc.psum_pool(name="psa", bufs=2))
         ctx.enter_context(tc.manual_schedule())
 
         xs = keep.tile([P, PACK], F32, name="xs")
@@ -59,6 +61,8 @@ def tile_graphaugmentation_pb_t_w8_kernel(
         dummy = keep.tile([P, 1], F32, name="dummy")
         nc.vector.memset(dummy[:], 0.0)
         nc.scalar.activation(out=dummy[:], in_=dummy[:], func=ACT.Sigmoid)
+        ident = keep.tile([P, P], BF16, name="ident")
+        make_identity(nc, ident[:])
 
         xb = [keep.tile([P, PACK, PIX], U8, name=f"xb{b}") for b in range(IMAGES)]
         ag = [keep.tile([P, PACK, PIX], BF16, name=f"ag{b}") for b in range(IMAGES)]
@@ -125,8 +129,11 @@ def tile_graphaugmentation_pb_t_w8_kernel(
                     in_=src[:, :, c0:c1].rearrange("p t (c i) -> p c t i", i=4),
                 )
 
+        def pool_copy(out, in_):
+            nc.gpsimd.tensor_scalar(out=out, in0=in_, scalar1=1.0, scalar2=0.0, op0=ALU.mult, op1=ALU.add)
+
         def x_pool(h):
-            return GX if 3 <= h and chunks[h][2] == N else 0
+            return min(GX if h >= 5 else GX // 2, chunks[h][2]) if h >= 3 else 0
 
         def width(h):
             return chunks[h][2]
@@ -183,11 +190,25 @@ def tile_graphaugmentation_pb_t_w8_kernel(
             b, px, n = chunks[h]
             nc.sync.dma_start(out=out_v[b][:, ts, px : px + n], in_=gt[h][:, ts, :])
 
+        ab = {}
+
+        def agg_psum(h):
+            b, px, n = chunks[h]
+            ab[h] = []
+            for u in range(2):
+                tile = psa.tile([P, 2, n], BF16, name="ab")
+                ab[h].append(tile)
+                for v in range(2):
+                    nc.tensor.matmul(
+                        out=tile[:, v, :], lhsT=ident[:], rhs=ag[b][:, 2 * u + v, px : px + n], start=True, stop=True
+                    )
+
         def prod(h, step):
-            src = part(ag, h)
             for t in range(0, PACK, step):
                 ts = slice(t, t + step)
-                nc.vector.tensor_tensor(out=gt[h][:, ts, :], in0=gt[h][:, ts, :], in1=src[:, ts, :], op=ALU.mult)
+                nc.vector.tensor_tensor(
+                    out=gt[h][:, ts, :], in0=ab[h][t // 2][:, t % 2 : t % 2 + step, :], in1=gt[h][:, ts, :], op=ALU.mult
+                )
                 if step == 1 and t % 2 == 1:
                     store(h, slice(t - 1, t + 1))
             if step > 1:
@@ -204,7 +225,7 @@ def tile_graphaugmentation_pb_t_w8_kernel(
                 if i >= 0:
                     mm1(i + 1)
             if on(i + 2):
-                widen(i + 2, (0, 1, 2), False)
+                widen(i + 2, range(PACK), False)
             if on(i):
                 hi[i] = grouped(i, work, "hi")
                 hs = width(i) // 2 if i >= count - 2 else 0
@@ -212,18 +233,20 @@ def tile_graphaugmentation_pb_t_w8_kernel(
                 inter(nc.scalar.copy, hi[i], hp[i], width(i) - hs, width(i))
             if on(i + 2):
                 xi[i + 2] = grouped(i + 2, work, "xi")
-                inter(nc.vector.tensor_copy, xi[i + 2], xw[i + 2], 0, width(i + 2))
+                inter(pool_copy, xi[i + 2], xw[i + 2], 0, x_pool(i + 2))
             if on(i + 1) and i >= 0:
                 relu(i + 1)
             if on(i + 3):
-                widen(i + 3, (3,), True)
                 ai[i + 3] = grouped(i + 3, deep, "ai")
                 inter(nc.scalar.copy, ai[i + 3], part(ag, i + 3), 0, width(i + 3))
+            if on(i - 1):
+                prod(i - 1, 1 if i >= count - 1 else 2)
             if on(i):
                 quant(hc, hsc, i, hi, "h")
                 mm2(i)
-            if on(i - 1):
-                prod(i - 1, 1 if i >= count - 1 else 4)
+                agg_psum(i)
+            if on(i + 2):
+                inter(nc.vector.tensor_copy, xi[i + 2], xw[i + 2], x_pool(i + 2), width(i + 2))
             if on(i + 2):
                 quant(xc, xsc, i + 2, xi, "x")
             if i == -1:

@@ -18,7 +18,7 @@ P = 128
 PACK = 4
 N = 512
 WIDTHS = [256, 256, 512] + [512] * 8 + [512, 256, 256]
-GX = 352
+GX = 320
 
 FLOPS = 2 * IMAGES * PIX * C * (2 * C + C)
 
@@ -129,8 +129,16 @@ def tile_graphaugmentation_pb_t_w8_kernel(
                     in_=src[:, :, c0:c1].rearrange("p t (c i) -> p c t i", i=4),
                 )
 
-        def pool_copy(out, in_):
-            nc.gpsimd.tensor_scalar(out=out, in0=in_, scalar1=1.0, scalar2=0.0, op0=ALU.mult, op1=ALU.add)
+        def pool_inter(dst, src, c1):
+            if c1:
+                nc.gpsimd.tensor_scalar(
+                    out=dst[:, :c1, :],
+                    in0=src[:, :, :c1].rearrange("p t c -> p c t"),
+                    scalar1=1.0,
+                    scalar2=0.0,
+                    op0=ALU.mult,
+                    op1=ALU.add,
+                )
 
         def x_pool(h):
             return min(GX if h >= 5 else GX // 2, chunks[h][2]) if h >= 3 else 0
@@ -233,7 +241,7 @@ def tile_graphaugmentation_pb_t_w8_kernel(
                 inter(nc.scalar.copy, hi[i], hp[i], width(i) - hs, width(i))
             if on(i + 2):
                 xi[i + 2] = grouped(i + 2, work, "xi")
-                inter(pool_copy, xi[i + 2], xw[i + 2], 0, x_pool(i + 2))
+                pool_inter(xi[i + 2], xw[i + 2], x_pool(i + 2))
             if on(i + 1) and i >= 0:
                 relu(i + 1)
             if on(i + 3):

@@ -17,8 +17,10 @@ IMAGES, C, PIX = 6, 512, 1024
 P = 128
 PACK = 4
 N = 512
-WIDTHS = [256, 256, 512] + [512] * 8 + [512, 256, 256]
-GX = 320
+WIDTHS = [256, 256] + [512] * 10 + [256, 256]
+COUNT = len(WIDTHS)
+S_SHARE = {COUNT - 2: 64, COUNT - 1: 64}
+STARTS = [sum(WIDTHS[:h]) for h in range(COUNT)]
 
 FLOPS = 2 * IMAGES * PIX * C * (2 * C + C)
 
@@ -31,20 +33,14 @@ def tile_graphaugmentation_pb_t_w8_kernel(
     agg_v = agg.rearrange("b (p t) h w -> b p t (h w)", t=PACK)
     out_v = out.rearrange("b (p t) h w -> b p t (h w)", t=PACK)
 
-    chunks = []
-    pos = 0
-    for n in WIDTHS:
-        chunks.append((pos // PIX, pos % PIX, n))
-        pos += n
-    count = len(chunks)
-
     with ExitStack() as ctx:
         keep = ctx.enter_context(tc.tile_pool(name="keep", bufs=1))
-        work = ctx.enter_context(tc.tile_pool(name="work", bufs=2))
-        deep = ctx.enter_context(tc.tile_pool(name="deep", bufs=3))
-        outs = ctx.enter_context(tc.tile_pool(name="outs", bufs=4))
-        psum = ctx.enter_context(tc.psum_pool(name="psum", bufs=6))
-        psa = ctx.enter_context(tc.psum_pool(name="psa", bufs=2))
+        two = ctx.enter_context(tc.tile_pool(name="two", bufs=2))
+        three = ctx.enter_context(tc.tile_pool(name="three", bufs=3))
+        four = ctx.enter_context(tc.tile_pool(name="four", bufs=4))
+        ps1 = ctx.enter_context(tc.psum_pool(name="ps1", bufs=2))
+        ps2 = ctx.enter_context(tc.psum_pool(name="ps2", bufs=2))
+        psa = ctx.enter_context(tc.psum_pool(name="psa", bufs=4))
         ctx.enter_context(tc.manual_schedule())
 
         xs = keep.tile([P, PACK], F32, name="xs")
@@ -100,27 +96,35 @@ def tile_graphaugmentation_pb_t_w8_kernel(
 
         def permute(dst, src):
             nc.vector.tensor_copy(
-                out=dst[:].rearrange("p (t m) -> p t m", t=PACK), in_=src[:].rearrange("p (m t) -> p t m", t=PACK)
+                out=dst[:].rearrange("p (t m) -> p m t", t=PACK), in_=src[:].rearrange("p (m t) -> p m t", t=PACK)
             )
 
-        xw, xi, ai, xc, xsc, ac, asc, hp, hi, hc, hsc, gt, acc1, acc2 = ({} for _ in range(14))
+        xw, xa, codes1, scales1, hp, hi, codes2, scales2, gt, ab, acc1, acc2 = ({} for _ in range(12))
 
-        def part(tiles, h):
-            b, px, n = chunks[h]
-            return tiles[b][:, :, px : px + n]
+        def where(h):
+            return STARTS[h] // PIX, slice(STARTS[h] % PIX, STARTS[h] % PIX + WIDTHS[h])
 
-        def widen(h, ts, scalar):
-            b, px, n = chunks[h]
-            if h not in xw:
-                xw[h] = work.tile([P, PACK, n], BF16, name="xw")
-            for t in ts:
-                src = xb[b][:, t, px : px + n].bitcast(FP8)
-                if scalar:
-                    nc.scalar.activation(out=xw[h][:, t, :], in_=src, func=ACT.Copy, scale=xs[:, t : t + 1])
-                else:
-                    nc.vector.tensor_scalar(
-                        out=xw[h][:, t, :], in0=src, scalar1=xs[:, t : t + 1], scalar2=None, op0=ALU.mult
-                    )
+        def scalar_planes(h):
+            return {0: 1, 1: 1, 2: 2}.get(h, h % 2)
+
+        def widen_scalar(h):
+            b, px = where(h)
+            xw[h] = two.tile([P, PACK, WIDTHS[h]], BF16, name="xw")
+            for t in range(PACK - scalar_planes(h), PACK):
+                nc.scalar.activation(
+                    out=xw[h][:, t, :], in_=xb[b][:, t, px].bitcast(FP8), func=ACT.Copy, scale=xs[:, t : t + 1]
+                )
+
+        def widen(h):
+            b, px = where(h)
+            for t in range(PACK - scalar_planes(h)):
+                nc.vector.tensor_scalar(
+                    out=xw[h][:, t, :],
+                    in0=xb[b][:, t, px].bitcast(FP8),
+                    scalar1=xs[:, t : t + 1],
+                    scalar2=None,
+                    op0=ALU.mult,
+                )
 
         def inter(copy, dst, src, c0, c1):
             if c1 > c0:
@@ -129,140 +133,159 @@ def tile_graphaugmentation_pb_t_w8_kernel(
                     in_=src[:, :, c0:c1].rearrange("p t (c i) -> p c t i", i=4),
                 )
 
-        def pool_inter(dst, src, c1):
-            if c1:
+        def pool_share(h):
+            return min(WIDTHS[h], 5 * WIDTHS[h - 5] // 8) if h >= 5 else 0
+
+        def inter_x_pool(h):
+            n = pool_share(h)
+            if n:
                 nc.gpsimd.tensor_scalar(
-                    out=dst[:, :c1, :],
-                    in0=src[:, :, :c1].rearrange("p t c -> p c t"),
+                    out=xa[h][:, 0, :n, :],
+                    in0=xw[h][:, :, :n].rearrange("p t c -> p c t"),
                     scalar1=1.0,
                     scalar2=0.0,
                     op0=ALU.mult,
                     op1=ALU.add,
                 )
 
-        def x_pool(h):
-            return min(GX if h >= 5 else GX // 2, chunks[h][2]) if h >= 3 else 0
+        def inter_x(h):
+            inter(nc.vector.tensor_copy, xa[h][:, 0, :, :], xw[h][:], pool_share(h), WIDTHS[h])
 
-        def width(h):
-            return chunks[h][2]
+        def inter_a(h, t):
+            b, px = where(h)
+            n = WIDTHS[h] // PACK
+            inter(nc.scalar.copy, xa[h][:, 1, :, :], ag[b][:, :, px], n * t, n * t + n)
 
-        def grouped(h, pool, name):
-            return pool.tile([P, width(h), PACK], BF16, name=name, align_bytes=64)
-
-        def quant(codes, scales, h, src, name):
-            n = width(h)
-            codes[h] = deep.tile([P, n], U32, name=name + "c", align_bytes=64)
-            scales[h] = deep.tile([P, n], U8, name=name + "s", align_bytes=64)
+        def quant_in(h):
+            n = WIDTHS[h]
+            codes1[h] = three.tile([P, 2, n], U32, name="codes1", align_bytes=64)
+            scales1[h] = three.tile([P, 2, n], U8, name="scales1", align_bytes=64)
             nc.vector.quantize_mx(
-                out=codes[h][:].bitcast(FP8X4), scales=scales[h][:], in_=src[h][:].rearrange("p n t -> p (n t)")
+                out=codes1[h][:].rearrange("p g n -> p (g n)").bitcast(FP8X4),
+                scales=scales1[h][:].rearrange("p g n -> p (g n)"),
+                in_=xa[h][:].rearrange("p g n t -> p (g n t)"),
             )
 
-        def product(acc, h, t, weights, planes, codes, scales, start, stop):
+        def inter_h_scalar(h):
+            n = WIDTHS[h]
+            hi[h] = two.tile([P, n, PACK], BF16, name="hi", align_bytes=64)
+            inter(nc.scalar.copy, hi[h], hp[h], n - S_SHARE.get(h, 0), n)
+
+        def inter_h(h):
+            n = WIDTHS[h]
+            inter(nc.vector.tensor_copy, hi[h], hp[h], 0, n - S_SHARE.get(h, 0))
+
+        def quant_h(h):
+            n = WIDTHS[h]
+            codes2[h] = two.tile([P, n], U32, name="codes2", align_bytes=64)
+            scales2[h] = two.tile([P, n], U8, name="scales2", align_bytes=64)
+            nc.vector.quantize_mx(
+                out=codes2[h][:].bitcast(FP8X4), scales=scales2[h][:], in_=hi[h][:].rearrange("p n t -> p (n t)")
+            )
+
+        def mm1(h, t):
             m = slice(P * t, P * t + P)
+            acc1[t] = ps1.tile([P, WIDTHS[h]], F32, name="acc1")
+            for g in range(2):
+                nc.tensor.matmul_mx(
+                    out=acc1[t][:],
+                    lhsT=w1[g][:, m].bitcast(FP8X4),
+                    lhsT_scale=s1[4 * g :, m],
+                    rhs=codes1[h][:, g, :].bitcast(FP8X4),
+                    rhs_scale=scales1[h][:, g, :],
+                    start=(g == 0),
+                    stop=(g == 1),
+                )
+
+        def mm2(h, t):
+            m = slice(P * t, P * t + P)
+            acc2[t] = ps2.tile([P, WIDTHS[h]], F32, name="acc2")
             nc.tensor.matmul_mx(
-                out=acc[:],
-                lhsT=weights[:, m].bitcast(FP8X4),
-                lhsT_scale=planes[:, m],
-                rhs=codes[h][:].bitcast(FP8X4),
-                rhs_scale=scales[h][:],
-                start=start,
-                stop=stop,
+                out=acc2[t][:],
+                lhsT=w2[:, m].bitcast(FP8X4),
+                lhsT_scale=s2[:, m],
+                rhs=codes2[h][:].bitcast(FP8X4),
+                rhs_scale=scales2[h][:],
+                start=True,
+                stop=True,
             )
 
-        def mm1(h):
-            acc1[h] = []
-            for t in range(PACK):
-                acc = psum.tile([P, width(h)], F32, name="acc")
-                acc1[h].append(acc)
-                product(acc, h, t, w1[0], s1[:], xc, xsc, True, False)
-                product(acc, h, t, w1[1], s1[4:, :], ac, asc, False, True)
+        def agg_psum(h, t):
+            b, px = where(h)
+            if t % 2 == 0:
+                ab[h, t // 2] = psa.tile([P, 2, WIDTHS[h]], BF16, name="ab")
+            nc.tensor.matmul(
+                out=ab[h, t // 2][:, t % 2, :], lhsT=ident[:], rhs=ag[b][:, t, px], start=True, stop=True
+            )
 
-        def mm2(h):
-            acc2[h] = []
-            for t in range(PACK):
-                acc = psum.tile([P, width(h)], F32, name="acc")
-                acc2[h].append(acc)
-                product(acc, h, t, w2, s2[:], hc, hsc, True, True)
+        def relu(h, t):
+            if t == 0:
+                hp[h] = two.tile([P, PACK, WIDTHS[h]], BF16, name="hp")
+            nc.scalar.activation(out=hp[h][:, t, :], in_=acc1[t][:], func=ACT.Relu, bias=b1[:, t : t + 1])
 
-        def relu(h):
-            hp[h] = work.tile([P, PACK, width(h)], BF16, name="hp")
-            for t in range(PACK):
-                nc.scalar.activation(out=hp[h][:, t, :], in_=acc1[h][t][:], func=ACT.Relu, bias=b1[:, t : t + 1])
-
-        def sig(h):
-            gt[h] = outs.tile([P, PACK, width(h)], F32, name="gt")
-            for t in range(PACK):
-                nc.scalar.activation(out=gt[h][:, t, :], in_=acc2[h][t][:], func=ACT.Sigmoid, bias=b2[:, t : t + 1])
-
-        def store(h, ts):
-            b, px, n = chunks[h]
-            nc.sync.dma_start(out=out_v[b][:, ts, px : px + n], in_=gt[h][:, ts, :])
-
-        ab = {}
-
-        def agg_psum(h):
-            b, px, n = chunks[h]
-            ab[h] = []
-            for u in range(2):
-                tile = psa.tile([P, 2, n], BF16, name="ab")
-                ab[h].append(tile)
-                for v in range(2):
-                    nc.tensor.matmul(
-                        out=tile[:, v, :], lhsT=ident[:], rhs=ag[b][:, 2 * u + v, px : px + n], start=True, stop=True
-                    )
+        def sig(h, t):
+            if t == 0:
+                gt[h] = four.tile([P, PACK, WIDTHS[h]], F32, name="gt")
+            nc.scalar.activation(out=gt[h][:, t, :], in_=acc2[t][:], func=ACT.Sigmoid, bias=b2[:, t : t + 1])
 
         def prod(h, step):
+            b, px = where(h)
             for t in range(0, PACK, step):
                 ts = slice(t, t + step)
                 nc.vector.tensor_tensor(
-                    out=gt[h][:, ts, :], in0=ab[h][t // 2][:, t % 2 : t % 2 + step, :], in1=gt[h][:, ts, :], op=ALU.mult
+                    out=gt[h][:, ts, :], in0=ab[h, t // 2][:, t % 2 : t % 2 + step, :], in1=gt[h][:, ts, :], op=ALU.mult
                 )
-                if step == 1 and t % 2 == 1:
-                    store(h, slice(t - 1, t + 1))
-            if step > 1:
-                store(h, slice(0, PACK))
+                if (t + step) % 2 == 0 and (h >= COUNT - 2 or t + step == PACK):
+                    t0 = t + step - 2 if h >= COUNT - 2 else 0
+                    nc.sync.dma_start(out=out_v[b][:, t0 : t + step, px], in_=gt[h][:, t0 : t + step, :])
 
         def on(h):
-            return 0 <= h < count
+            return 0 <= h < COUNT
 
-        for i in range(-3, count + 1):
-            if on(i - 1):
-                sig(i - 1)
-            if on(i + 1):
-                quant(ac, asc, i + 1, ai, "a")
-                if i >= 0:
-                    mm1(i + 1)
-            if on(i + 2):
-                widen(i + 2, range(PACK), False)
-            if on(i):
-                hi[i] = grouped(i, work, "hi")
-                hs = width(i) // 2 if i >= count - 2 else 0
-                inter(nc.vector.tensor_copy, hi[i], hp[i], 0, width(i) - hs)
-                inter(nc.scalar.copy, hi[i], hp[i], width(i) - hs, width(i))
-            if on(i + 2):
-                xi[i + 2] = grouped(i + 2, work, "xi")
-                pool_inter(xi[i + 2], xw[i + 2], x_pool(i + 2))
-            if on(i + 1) and i >= 0:
-                relu(i + 1)
+        for i in range(-3, COUNT + 2):
+            tail = i >= COUNT - 1
             if on(i + 3):
-                ai[i + 3] = grouped(i + 3, deep, "ai")
-                inter(nc.scalar.copy, ai[i + 3], part(ag, i + 3), 0, width(i + 3))
-            if on(i - 1):
-                prod(i - 1, 1 if i >= count - 1 else 2)
+                xa[i + 3] = three.tile([P, 2, WIDTHS[i + 3], PACK], BF16, name="xa", align_bytes=64)
+                widen_scalar(i + 3)
             if on(i):
-                quant(hc, hsc, i, hi, "h")
-                mm2(i)
-                agg_psum(i)
-            if on(i + 2):
-                inter(nc.vector.tensor_copy, xi[i + 2], xw[i + 2], x_pool(i + 2), width(i + 2))
-            if on(i + 2):
-                quant(xc, xsc, i + 2, xi, "x")
-            if i == -1:
+                inter_h_scalar(i)
+            for t in range(PACK):
+                if on(i + 1) and i >= 0:
+                    mm1(i + 1, t)
+                if on(i - 1):
+                    mm2(i - 1, t)
+                    agg_psum(i - 1, t)
+                if on(i + 1) and i >= 0:
+                    relu(i + 1, t)
+                if on(i - 1):
+                    sig(i - 1, t)
+                if on(i + 3):
+                    inter_a(i + 3, t)
+            if on(i + 3):
+                widen(i + 3)
+            if on(i + 2) and i >= 0:
+                quant_in(i + 2)
+            if on(i):
+                inter_h(i)
+            if on(i + 3):
+                inter_x_pool(i + 3)
+            if on(i - 2) and not tail:
+                prod(i - 2, 2)
+            if on(i):
+                quant_h(i)
+            if on(i - 2) and tail:
+                prod(i - 2, 1 if i == COUNT + 1 else 2)
+            if on(i + 3):
+                inter_x(i + 3)
+            if on(i + 2) and i < 0:
+                quant_in(i + 2)
+            if i == -2:
                 permute(s1, s1_raw)
                 permute(w1[0], w1_raw[0])
                 permute(w1[1], w1_raw[1])
-                mm1(0)
-                relu(0)
             if i == -1:
+                for t in range(PACK):
+                    mm1(0, t)
+                    relu(0, t)
                 permute(s2, s2_raw)
                 permute(w2, w2_raw)

@@ -1,7 +1,6 @@
 from contextlib import ExitStack
 
 import concourse.mybir as mybir
-from concourse.masks import make_identity
 
 F32 = mybir.dt.float32
 BF16 = mybir.dt.bfloat16
@@ -17,9 +16,10 @@ IMAGES, C, PIX = 6, 512, 1024
 P = 128
 PACK = 4
 N = 512
-WIDTHS = [256, 256] + [512] * 10 + [256, 256]
+WIDTHS = [256, 512, 256] + [512] * 9 + [256, 256]
 COUNT = len(WIDTHS)
-S_SHARE = {COUNT - 2: 64, COUNT - 1: 64}
+S_SHARE_H = {COUNT - 3: 128, COUNT - 2: 128, COUNT - 1: 128}
+S_SHARE_X = 128
 STARTS = [sum(WIDTHS[:h]) for h in range(COUNT)]
 
 FLOPS = 2 * IMAGES * PIX * C * (2 * C + C)
@@ -38,9 +38,8 @@ def tile_graphaugmentation_pb_t_w8_kernel(
         two = ctx.enter_context(tc.tile_pool(name="two", bufs=2))
         three = ctx.enter_context(tc.tile_pool(name="three", bufs=3))
         four = ctx.enter_context(tc.tile_pool(name="four", bufs=4))
-        ps1 = ctx.enter_context(tc.psum_pool(name="ps1", bufs=2))
-        ps2 = ctx.enter_context(tc.psum_pool(name="ps2", bufs=2))
-        psa = ctx.enter_context(tc.psum_pool(name="psa", bufs=4))
+        ps1 = ctx.enter_context(tc.psum_pool(name="ps1", bufs=4))
+        ps2 = ctx.enter_context(tc.psum_pool(name="ps2", bufs=4))
         ctx.enter_context(tc.manual_schedule())
 
         xs = keep.tile([P, PACK], F32, name="xs")
@@ -57,8 +56,6 @@ def tile_graphaugmentation_pb_t_w8_kernel(
         dummy = keep.tile([P, 1], F32, name="dummy")
         nc.vector.memset(dummy[:], 0.0)
         nc.scalar.activation(out=dummy[:], in_=dummy[:], func=ACT.Sigmoid)
-        ident = keep.tile([P, P], BF16, name="ident")
-        make_identity(nc, ident[:])
 
         xb = [keep.tile([P, PACK, PIX], U8, name=f"xb{b}") for b in range(IMAGES)]
         ag = [keep.tile([P, PACK, PIX], BF16, name=f"ag{b}") for b in range(IMAGES)]
@@ -73,14 +70,14 @@ def tile_graphaugmentation_pb_t_w8_kernel(
             nc.sync.dma_start(out=ag[b][:, :, px], in_=agg_v[b][:, :, px])
 
         load(0, slice(0, 256))
-        load(0, slice(256, 512))
+        load(0, slice(256, 768))
         for q in range(4):
             nc.sync.dma_start(
                 out=s1_raw[32 * q : 32 * q + 8, :].bitcast(I32), in_=g1w_scales[:, 4 * q : 4 * q + 4, :].bitcast(I32)
             )
         nc.sync.dma_start(out=w1_raw[0][:], in_=words(g1w_words[0]))
         nc.sync.dma_start(out=w1_raw[1][:], in_=words(g1w_words[1]))
-        load(0, slice(512, PIX))
+        load(0, slice(768, PIX))
         for q in range(4):
             nc.sync.dma_start(
                 out=s2_raw[32 * q : 32 * q + 4, :].bitcast(I32), in_=g2w_scales[0, 4 * q : 4 * q + 4, :].bitcast(I32)
@@ -99,193 +96,164 @@ def tile_graphaugmentation_pb_t_w8_kernel(
                 out=dst[:].rearrange("p (t m) -> p m t", t=PACK), in_=src[:].rearrange("p (m t) -> p m t", t=PACK)
             )
 
-        xw, xa, codes1, scales1, hp, hi, codes2, scales2, gt, ab, acc1, acc2 = ({} for _ in range(12))
+        xw, xa, codes1, scales1, hp, hi, codes2, scales2, gt, acc1, acc2 = ({} for _ in range(11))
 
         def where(h):
             return STARTS[h] // PIX, slice(STARTS[h] % PIX, STARTS[h] % PIX + WIDTHS[h])
 
-        def scalar_planes(h):
-            return {0: 1, 1: 1, 2: 2}.get(h, h % 2)
-
-        def widen_scalar(h):
-            b, px = where(h)
-            xw[h] = two.tile([P, PACK, WIDTHS[h]], BF16, name="xw")
-            for t in range(PACK - scalar_planes(h), PACK):
-                nc.scalar.activation(
-                    out=xw[h][:, t, :], in_=xb[b][:, t, px].bitcast(FP8), func=ACT.Copy, scale=xs[:, t : t + 1]
-                )
-
         def widen(h):
             b, px = where(h)
-            for t in range(PACK - scalar_planes(h)):
+            xw[h] = two.tile([P, 2, 2 * WIDTHS[h]], BF16, name="xw")
+            for t in range(PACK):
                 nc.vector.tensor_scalar(
-                    out=xw[h][:, t, :],
+                    out=xw[h][:, t // 2, t % 2 :: 2],
                     in0=xb[b][:, t, px].bitcast(FP8),
                     scalar1=xs[:, t : t + 1],
                     scalar2=None,
                     op0=ALU.mult,
                 )
 
+        def join(copy, h, c0, c1):
+            if c1 > c0:
+                copy(
+                    out=xa[h][:, 0, PACK * c0 : PACK * c1].bitcast(F32).rearrange("p (c u) -> p c u", u=2),
+                    in_=xw[h][:, :, 2 * c0 : 2 * c1].bitcast(F32).rearrange("p u c -> p c u"),
+                )
+
+        def x_split(h):
+            return WIDTHS[h] - (S_SHARE_X if h > 2 and WIDTHS[h] == N else 0)
+
         def inter(copy, dst, src, c0, c1):
             if c1 > c0:
                 copy(
-                    out=dst[:, c0:c1, :].rearrange("p (c i) t -> p c t i", i=4),
+                    out=dst[:, PACK * c0 : PACK * c1].rearrange("p (c i t) -> p c t i", i=4, t=PACK),
                     in_=src[:, :, c0:c1].rearrange("p t (c i) -> p c t i", i=4),
                 )
 
-        def pool_share(h):
-            return min(WIDTHS[h], 5 * WIDTHS[h - 5] // 8) if h >= 5 else 0
-
-        def inter_x_pool(h):
-            n = pool_share(h)
-            if n:
-                nc.gpsimd.tensor_scalar(
-                    out=xa[h][:, 0, :n, :],
-                    in0=xw[h][:, :, :n].rearrange("p t c -> p c t"),
-                    scalar1=1.0,
-                    scalar2=0.0,
-                    op0=ALU.mult,
-                    op1=ALU.add,
-                )
-
-        def inter_x(h):
-            inter(nc.vector.tensor_copy, xa[h][:, 0, :, :], xw[h][:], pool_share(h), WIDTHS[h])
-
-        def inter_a(h, t):
+        def inter_a(h):
             b, px = where(h)
-            n = WIDTHS[h] // PACK
-            inter(nc.scalar.copy, xa[h][:, 1, :, :], ag[b][:, :, px], n * t, n * t + n)
+            xa[h] = three.tile([P, 2, PACK * WIDTHS[h]], BF16, name="xa", align_bytes=64)
+            inter(nc.scalar.copy, xa[h][:, 1, :], ag[b][:, :, px], 0, WIDTHS[h])
 
         def quant_in(h):
             n = WIDTHS[h]
-            codes1[h] = three.tile([P, 2, n], U32, name="codes1", align_bytes=64)
-            scales1[h] = three.tile([P, 2, n], U8, name="scales1", align_bytes=64)
+            codes1[h] = two.tile([P, 2, n], U32, name="codes1", align_bytes=64)
+            scales1[h] = two.tile([P, 2, n], U8, name="scales1", align_bytes=64)
             nc.vector.quantize_mx(
                 out=codes1[h][:].rearrange("p g n -> p (g n)").bitcast(FP8X4),
                 scales=scales1[h][:].rearrange("p g n -> p (g n)"),
-                in_=xa[h][:].rearrange("p g n t -> p (g n t)"),
+                in_=xa[h][:].rearrange("p g m -> p (g m)"),
             )
 
-        def inter_h_scalar(h):
-            n = WIDTHS[h]
-            hi[h] = two.tile([P, n, PACK], BF16, name="hi", align_bytes=64)
-            inter(nc.scalar.copy, hi[h], hp[h], n - S_SHARE.get(h, 0), n)
+        def h_split(h):
+            return WIDTHS[h] - S_SHARE_H.get(h, 0)
 
-        def inter_h(h):
-            n = WIDTHS[h]
-            inter(nc.vector.tensor_copy, hi[h], hp[h], 0, n - S_SHARE.get(h, 0))
+        def inter_h_scalar(h):
+            hi[h] = two.tile([P, PACK * WIDTHS[h]], BF16, name="hi", align_bytes=64)
+            inter(nc.scalar.copy, hi[h], hp[h], h_split(h), WIDTHS[h])
+
+        def inter_h_vector(h):
+            inter(nc.vector.tensor_copy, hi[h], hp[h], 0, h_split(h))
 
         def quant_h(h):
             n = WIDTHS[h]
             codes2[h] = two.tile([P, n], U32, name="codes2", align_bytes=64)
             scales2[h] = two.tile([P, n], U8, name="scales2", align_bytes=64)
-            nc.vector.quantize_mx(
-                out=codes2[h][:].bitcast(FP8X4), scales=scales2[h][:], in_=hi[h][:].rearrange("p n t -> p (n t)")
-            )
+            nc.vector.quantize_mx(out=codes2[h][:].bitcast(FP8X4), scales=scales2[h][:], in_=hi[h][:])
 
-        def mm1(h, t):
-            m = slice(P * t, P * t + P)
-            acc1[t] = ps1.tile([P, WIDTHS[h]], F32, name="acc1")
-            for g in range(2):
+        def mm1(h):
+            for t in range(PACK):
+                m = slice(P * t, P * t + P)
+                acc1[h, t] = ps1.tile([P, WIDTHS[h]], F32, name="acc1")
+                for g in range(2):
+                    nc.tensor.matmul_mx(
+                        out=acc1[h, t][:],
+                        lhsT=w1[g][:, m].bitcast(FP8X4),
+                        lhsT_scale=s1[4 * g :, m],
+                        rhs=codes1[h][:, g, :].bitcast(FP8X4),
+                        rhs_scale=scales1[h][:, g, :],
+                        start=(g == 0),
+                        stop=(g == 1),
+                    )
+
+        def mm2(h):
+            for t in range(PACK):
+                m = slice(P * t, P * t + P)
+                acc2[h, t] = ps2.tile([P, WIDTHS[h]], F32, name="acc2")
                 nc.tensor.matmul_mx(
-                    out=acc1[t][:],
-                    lhsT=w1[g][:, m].bitcast(FP8X4),
-                    lhsT_scale=s1[4 * g :, m],
-                    rhs=codes1[h][:, g, :].bitcast(FP8X4),
-                    rhs_scale=scales1[h][:, g, :],
-                    start=(g == 0),
-                    stop=(g == 1),
+                    out=acc2[h, t][:],
+                    lhsT=w2[:, m].bitcast(FP8X4),
+                    lhsT_scale=s2[:, m],
+                    rhs=codes2[h][:].bitcast(FP8X4),
+                    rhs_scale=scales2[h][:],
+                    start=True,
+                    stop=True,
                 )
 
-        def mm2(h, t):
-            m = slice(P * t, P * t + P)
-            acc2[t] = ps2.tile([P, WIDTHS[h]], F32, name="acc2")
-            nc.tensor.matmul_mx(
-                out=acc2[t][:],
-                lhsT=w2[:, m].bitcast(FP8X4),
-                lhsT_scale=s2[:, m],
-                rhs=codes2[h][:].bitcast(FP8X4),
-                rhs_scale=scales2[h][:],
-                start=True,
-                stop=True,
-            )
+        def relu(h):
+            hp[h] = two.tile([P, PACK, WIDTHS[h]], BF16, name="hp")
+            for t in range(PACK):
+                nc.scalar.activation(out=hp[h][:, t, :], in_=acc1[h, t][:], func=ACT.Relu, bias=b1[:, t : t + 1])
 
-        def agg_psum(h, t):
+        def sig(h):
+            gt[h] = four.tile([P, PACK, WIDTHS[h]], F32, name="gt")
+            for t in range(PACK):
+                nc.scalar.activation(out=gt[h][:, t, :], in_=acc2[h, t][:], func=ACT.Sigmoid, bias=b2[:, t : t + 1])
+
+        def prod(h):
             b, px = where(h)
-            if t % 2 == 0:
-                ab[h, t // 2] = psa.tile([P, 2, WIDTHS[h]], BF16, name="ab")
-            nc.tensor.matmul(
-                out=ab[h, t // 2][:, t % 2, :], lhsT=ident[:], rhs=ag[b][:, t, px], start=True, stop=True
-            )
-
-        def relu(h, t):
-            if t == 0:
-                hp[h] = two.tile([P, PACK, WIDTHS[h]], BF16, name="hp")
-            nc.scalar.activation(out=hp[h][:, t, :], in_=acc1[t][:], func=ACT.Relu, bias=b1[:, t : t + 1])
-
-        def sig(h, t):
-            if t == 0:
-                gt[h] = four.tile([P, PACK, WIDTHS[h]], F32, name="gt")
-            nc.scalar.activation(out=gt[h][:, t, :], in_=acc2[t][:], func=ACT.Sigmoid, bias=b2[:, t : t + 1])
-
-        def prod(h, step):
-            b, px = where(h)
+            step = 1 if h >= COUNT - 2 else PACK
             for t in range(0, PACK, step):
                 ts = slice(t, t + step)
-                nc.vector.tensor_tensor(
-                    out=gt[h][:, ts, :], in0=ab[h, t // 2][:, t % 2 : t % 2 + step, :], in1=gt[h][:, ts, :], op=ALU.mult
-                )
-                if (t + step) % 2 == 0 and (h >= COUNT - 2 or t + step == PACK):
-                    t0 = t + step - 2 if h >= COUNT - 2 else 0
-                    nc.sync.dma_start(out=out_v[b][:, t0 : t + step, px], in_=gt[h][:, t0 : t + step, :])
+                nc.vector.tensor_tensor(out=gt[h][:, ts, :], in0=gt[h][:, ts, :], in1=ag[b][:, ts, px], op=ALU.mult)
+                if step == PACK or t % 2 == 1:
+                    ts = slice(0, PACK) if step == PACK else slice(t - 1, t + 1)
+                    nc.sync.dma_start(out=out_v[b][:, ts, px], in_=gt[h][:, ts, :])
 
         def on(h):
             return 0 <= h < COUNT
 
-        for i in range(-3, COUNT + 2):
-            tail = i >= COUNT - 1
-            if on(i + 3):
-                xa[i + 3] = three.tile([P, 2, WIDTHS[i + 3], PACK], BF16, name="xa", align_bytes=64)
-                widen_scalar(i + 3)
+        inter_a(0)
+        widen(0)
+        join(nc.vector.tensor_copy, 0, 0, WIDTHS[0])
+        inter_a(1)
+        widen(1)
+        quant_in(0)
+        permute(s1, s1_raw)
+        permute(w1[0], w1_raw[0])
+        permute(w1[1], w1_raw[1])
+        join(nc.vector.tensor_copy, 1, 0, WIDTHS[1])
+        mm1(0)
+        relu(0)
+        inter_a(2)
+        for i in range(COUNT + 1):
             if on(i):
                 inter_h_scalar(i)
-            for t in range(PACK):
-                if on(i + 1) and i >= 0:
-                    mm1(i + 1, t)
-                if on(i - 1):
-                    mm2(i - 1, t)
-                    agg_psum(i - 1, t)
-                if on(i + 1) and i >= 0:
-                    relu(i + 1, t)
-                if on(i - 1):
-                    sig(i - 1, t)
-                if on(i + 3):
-                    inter_a(i + 3, t)
-            if on(i + 3):
-                widen(i + 3)
-            if on(i + 2) and i >= 0:
-                quant_in(i + 2)
+            if on(i - 1):
+                sig(i - 1)
+            if on(i + 1):
+                quant_in(i + 1)
+                mm1(i + 1)
+            if i == 0:
+                relu(1)
+                widen(2)
             if on(i):
-                inter_h(i)
+                inter_h_vector(i)
+            if on(i + 2) and i > 0:
+                widen(i + 2)
             if on(i + 3):
-                inter_x_pool(i + 3)
-            if on(i - 2) and not tail:
-                prod(i - 2, 2)
-            if on(i):
-                quant_h(i)
-            if on(i - 2) and tail:
-                prod(i - 2, 1 if i == COUNT + 1 else 2)
-            if on(i + 3):
-                inter_x(i + 3)
-            if on(i + 2) and i < 0:
-                quant_in(i + 2)
-            if i == -2:
-                permute(s1, s1_raw)
-                permute(w1[0], w1_raw[0])
-                permute(w1[1], w1_raw[1])
-            if i == -1:
-                for t in range(PACK):
-                    mm1(0, t)
-                    relu(0, t)
+                inter_a(i + 3)
+            if on(i + 2):
+                join(nc.scalar.copy, i + 2, x_split(i + 2), WIDTHS[i + 2])
+            if on(i + 1) and i > 0:
+                relu(i + 1)
+            if i == 0:
                 permute(s2, s2_raw)
                 permute(w2, w2_raw)
+            if on(i):
+                quant_h(i)
+                mm2(i)
+            if on(i + 2):
+                join(nc.vector.tensor_copy, i + 2, 0, x_split(i + 2))
+            if on(i - 1):
+                prod(i - 1)

from contextlib import ExitStack

import concourse.mybir as mybir

F32 = mybir.dt.float32
BF16 = mybir.dt.bfloat16
I32 = mybir.dt.int32
U32 = mybir.dt.uint32
U8 = mybir.dt.uint8
FP8 = mybir.dt.float8_e4m3fn
FP8X4 = mybir.dt.float8_e4m3fn_x4
ACT = mybir.ActivationFunctionType
ALU = mybir.AluOpType

IMAGES, C, PIX = 6, 512, 1024
P = 128
PACK = 4
N = 512
WIDTHS = [256, 512, 256] + [512] * 9 + [256, 256]
COUNT = len(WIDTHS)
S_SHARE_H = {COUNT - 3: 128, COUNT - 2: 128, COUNT - 1: 128}
S_SHARE_X = 128
STARTS = [sum(WIDTHS[:h]) for h in range(COUNT)]

FLOPS = 2 * IMAGES * PIX * C * (2 * C + C)


def tile_graphaugmentation_pb_t_w8_kernel(
    tc, x_bytes, x_scale, agg, g1w_words, g1w_scales, g1b, g2w_words, g2w_scales, g2b, out
):
    nc = tc.nc
    x_v = x_bytes.rearrange("b (p t) h w -> b p t (h w)", t=PACK)
    agg_v = agg.rearrange("b (p t) h w -> b p t (h w)", t=PACK)
    out_v = out.rearrange("b (p t) h w -> b p t (h w)", t=PACK)

    with ExitStack() as ctx:
        keep = ctx.enter_context(tc.tile_pool(name="keep", bufs=1))
        two = ctx.enter_context(tc.tile_pool(name="two", bufs=2))
        three = ctx.enter_context(tc.tile_pool(name="three", bufs=3))
        four = ctx.enter_context(tc.tile_pool(name="four", bufs=4))
        ps1 = ctx.enter_context(tc.psum_pool(name="ps1", bufs=4))
        ps2 = ctx.enter_context(tc.psum_pool(name="ps2", bufs=4))
        ctx.enter_context(tc.manual_schedule())

        xs = keep.tile([P, PACK], F32, name="xs")
        b1 = keep.tile([P, PACK], BF16, name="b1")
        b2 = keep.tile([P, PACK], BF16, name="b2")
        nc.scalar.dma_start(out=xs[:], in_=x_scale.rearrange("o (p t) h w -> p (o t h w)", t=PACK))
        nc.gpsimd.dma_start(out=b1[:], in_=g1b.rearrange("(p t) -> p t", t=PACK))
        nc.gpsimd.dma_start(out=b2[:], in_=g2b.rearrange("(p t) -> p t", t=PACK))

        s1_raw = keep.tile([P, C], U8, name="s1_raw", align_bytes=64)
        s2_raw = keep.tile([P, C], U8, name="s2_raw", align_bytes=64)
        nc.vector.memset(s1_raw[:].bitcast(I32), 0)
        nc.vector.memset(s2_raw[:].bitcast(I32), 0)
        dummy = keep.tile([P, 1], F32, name="dummy")
        nc.vector.memset(dummy[:], 0.0)
        nc.scalar.activation(out=dummy[:], in_=dummy[:], func=ACT.Sigmoid)

        xb = [keep.tile([P, PACK, PIX], U8, name=f"xb{b}") for b in range(IMAGES)]
        ag = [keep.tile([P, PACK, PIX], BF16, name=f"ag{b}") for b in range(IMAGES)]
        w1_raw = [keep.tile([P, C], I32, name=f"w1_raw{g}", align_bytes=64) for g in range(2)]
        w2_raw = keep.tile([P, C], I32, name="w2_raw", align_bytes=64)

        def words(src):
            return src.rearrange("p n t -> p (n t)").bitcast(I32)

        def load(b, px):
            nc.sync.dma_start(out=xb[b][:, :, px], in_=x_v[b][:, :, px])
            nc.sync.dma_start(out=ag[b][:, :, px], in_=agg_v[b][:, :, px])

        load(0, slice(0, 256))
        load(0, slice(256, 768))
        for q in range(4):
            nc.sync.dma_start(
                out=s1_raw[32 * q : 32 * q + 8, :].bitcast(I32), in_=g1w_scales[:, 4 * q : 4 * q + 4, :].bitcast(I32)
            )
        nc.sync.dma_start(out=w1_raw[0][:], in_=words(g1w_words[0]))
        nc.sync.dma_start(out=w1_raw[1][:], in_=words(g1w_words[1]))
        load(0, slice(768, PIX))
        for q in range(4):
            nc.sync.dma_start(
                out=s2_raw[32 * q : 32 * q + 4, :].bitcast(I32), in_=g2w_scales[0, 4 * q : 4 * q + 4, :].bitcast(I32)
            )
        nc.sync.dma_start(out=w2_raw[:], in_=words(g2w_words[0]))
        for b in range(1, IMAGES):
            load(b, slice(0, PIX))

        w1 = [keep.tile([P, C], I32, name=f"w1_{g}", align_bytes=64) for g in range(2)]
        w2 = keep.tile([P, C], I32, name="w2", align_bytes=64)
        s1 = keep.tile([P, C], U8, name="s1", align_bytes=64)
        s2 = keep.tile([P, C], U8, name="s2", align_bytes=64)

        def permute(dst, src):
            nc.vector.tensor_copy(
                out=dst[:].rearrange("p (t m) -> p m t", t=PACK), in_=src[:].rearrange("p (m t) -> p m t", t=PACK)
            )

        xw, xa, codes1, scales1, hp, hi, codes2, scales2, gt, acc1, acc2 = ({} for _ in range(11))

        def where(h):
            return STARTS[h] // PIX, slice(STARTS[h] % PIX, STARTS[h] % PIX + WIDTHS[h])

        def widen(h):
            b, px = where(h)
            xw[h] = two.tile([P, 2, 2 * WIDTHS[h]], BF16, name="xw")
            for t in range(PACK):
                nc.vector.tensor_scalar(
                    out=xw[h][:, t // 2, t % 2 :: 2],
                    in0=xb[b][:, t, px].bitcast(FP8),
                    scalar1=xs[:, t : t + 1],
                    scalar2=None,
                    op0=ALU.mult,
                )

        def join(copy, h, c0, c1):
            if c1 > c0:
                copy(
                    out=xa[h][:, 0, PACK * c0 : PACK * c1].bitcast(F32).rearrange("p (c u) -> p c u", u=2),
                    in_=xw[h][:, :, 2 * c0 : 2 * c1].bitcast(F32).rearrange("p u c -> p c u"),
                )

        def x_split(h):
            return WIDTHS[h] - (S_SHARE_X if h > 2 and WIDTHS[h] == N else 0)

        def inter(copy, dst, src, c0, c1):
            if c1 > c0:
                copy(
                    out=dst[:, PACK * c0 : PACK * c1].rearrange("p (c i t) -> p c t i", i=4, t=PACK),
                    in_=src[:, :, c0:c1].rearrange("p t (c i) -> p c t i", i=4),
                )

        def inter_a(h):
            b, px = where(h)
            xa[h] = three.tile([P, 2, PACK * WIDTHS[h]], BF16, name="xa", align_bytes=64)
            inter(nc.scalar.copy, xa[h][:, 1, :], ag[b][:, :, px], 0, WIDTHS[h])

        def quant_in(h):
            n = WIDTHS[h]
            codes1[h] = two.tile([P, 2, n], U32, name="codes1", align_bytes=64)
            scales1[h] = two.tile([P, 2, n], U8, name="scales1", align_bytes=64)
            nc.vector.quantize_mx(
                out=codes1[h][:].rearrange("p g n -> p (g n)").bitcast(FP8X4),
                scales=scales1[h][:].rearrange("p g n -> p (g n)"),
                in_=xa[h][:].rearrange("p g m -> p (g m)"),
            )

        def h_split(h):
            return WIDTHS[h] - S_SHARE_H.get(h, 0)

        def inter_h_scalar(h):
            hi[h] = two.tile([P, PACK * WIDTHS[h]], BF16, name="hi", align_bytes=64)
            inter(nc.scalar.copy, hi[h], hp[h], h_split(h), WIDTHS[h])

        def inter_h_vector(h):
            inter(nc.vector.tensor_copy, hi[h], hp[h], 0, h_split(h))

        def quant_h(h):
            n = WIDTHS[h]
            codes2[h] = two.tile([P, n], U32, name="codes2", align_bytes=64)
            scales2[h] = two.tile([P, n], U8, name="scales2", align_bytes=64)
            nc.vector.quantize_mx(out=codes2[h][:].bitcast(FP8X4), scales=scales2[h][:], in_=hi[h][:])

        def mm1(h):
            for t in range(PACK):
                m = slice(P * t, P * t + P)
                acc1[h, t] = ps1.tile([P, WIDTHS[h]], F32, name="acc1")
                for g in range(2):
                    nc.tensor.matmul_mx(
                        out=acc1[h, t][:],
                        lhsT=w1[g][:, m].bitcast(FP8X4),
                        lhsT_scale=s1[4 * g :, m],
                        rhs=codes1[h][:, g, :].bitcast(FP8X4),
                        rhs_scale=scales1[h][:, g, :],
                        start=(g == 0),
                        stop=(g == 1),
                    )

        def mm2(h):
            for t in range(PACK):
                m = slice(P * t, P * t + P)
                acc2[h, t] = ps2.tile([P, WIDTHS[h]], F32, name="acc2")
                nc.tensor.matmul_mx(
                    out=acc2[h, t][:],
                    lhsT=w2[:, m].bitcast(FP8X4),
                    lhsT_scale=s2[:, m],
                    rhs=codes2[h][:].bitcast(FP8X4),
                    rhs_scale=scales2[h][:],
                    start=True,
                    stop=True,
                )

        def relu(h):
            hp[h] = two.tile([P, PACK, WIDTHS[h]], BF16, name="hp")
            for t in range(PACK):
                nc.scalar.activation(out=hp[h][:, t, :], in_=acc1[h, t][:], func=ACT.Relu, bias=b1[:, t : t + 1])

        def sig(h):
            gt[h] = four.tile([P, PACK, WIDTHS[h]], F32, name="gt")
            for t in range(PACK):
                nc.scalar.activation(out=gt[h][:, t, :], in_=acc2[h, t][:], func=ACT.Sigmoid, bias=b2[:, t : t + 1])

        def prod(h):
            b, px = where(h)
            step = 1 if h >= COUNT - 2 else PACK
            for t in range(0, PACK, step):
                ts = slice(t, t + step)
                nc.vector.tensor_tensor(out=gt[h][:, ts, :], in0=gt[h][:, ts, :], in1=ag[b][:, ts, px], op=ALU.mult)
                if step == PACK or t % 2 == 1:
                    ts = slice(0, PACK) if step == PACK else slice(t - 1, t + 1)
                    nc.sync.dma_start(out=out_v[b][:, ts, px], in_=gt[h][:, ts, :])

        def on(h):
            return 0 <= h < COUNT

        inter_a(0)
        widen(0)
        join(nc.vector.tensor_copy, 0, 0, WIDTHS[0])
        inter_a(1)
        widen(1)
        quant_in(0)
        permute(s1, s1_raw)
        permute(w1[0], w1_raw[0])
        permute(w1[1], w1_raw[1])
        join(nc.vector.tensor_copy, 1, 0, WIDTHS[1])
        mm1(0)
        relu(0)
        inter_a(2)
        for i in range(COUNT + 1):
            if on(i):
                inter_h_scalar(i)
            if on(i - 1):
                sig(i - 1)
            if on(i + 1):
                quant_in(i + 1)
                mm1(i + 1)
            if i == 0:
                relu(1)
                widen(2)
            if on(i):
                inter_h_vector(i)
            if on(i + 2) and i > 0:
                widen(i + 2)
            if on(i + 3):
                inter_a(i + 3)
            if on(i + 2):
                join(nc.scalar.copy, i + 2, x_split(i + 2), WIDTHS[i + 2])
            if on(i + 1) and i > 0:
                relu(i + 1)
            if i == 0:
                permute(s2, s2_raw)
                permute(w2, w2_raw)
            if on(i):
                quant_h(i)
                mm2(i)
            if on(i + 2):
                join(nc.vector.tensor_copy, i + 2, 0, x_split(i + 2))
            if on(i - 1):
                prod(i - 1)
